import numpy as np
import ml_dtypes


def mxq(x, axis, fmt="e4m3"):
    dtype, down = {"e4m3": (ml_dtypes.float8_e4m3fn, 7), "e5m2": (ml_dtypes.float8_e5m2, 14)}[fmt]
    v = np.moveaxis(np.asarray(x, np.float32).astype(ml_dtypes.bfloat16).astype(np.float64), axis, -1)
    blocks = v.reshape(v.shape[:-1] + (-1, 32))
    amax = np.abs(blocks).max(-1, keepdims=True)
    byte = np.maximum(np.where(amax > 0, np.frexp(amax)[1] - 1 + 127, 0) - down, 1)
    scale = np.exp2(byte - 127.0)
    codes = (blocks / scale).astype(np.float32).astype(dtype).astype(np.float64)
    return np.moveaxis((codes * scale).reshape(v.shape), -1, axis)


WIDE = False


def mx_kscale(k):
    if not WIDE:
        return np.ones(k)
    levels = np.array([10, -10, 5, -5, 0])
    a = np.random.permutation(np.resize(levels, k // 512 * 4)).reshape(k // 512, 4)
    idx = np.arange(k)
    return np.exp2(a[idx // 512, idx % 128 // 32])


BF16 = ml_dtypes.bfloat16


def bf(x):
    return np.asarray(x, np.float32).astype(BF16)


def f64(x):
    return np.asarray(x).astype(np.float64)


E2M1 = np.array([0.0, 0.5, 1.0, 1.5, 2.0, 3.0, 4.0, 6.0, -0.0, -0.5, -1.0, -1.5, -2.0, -3.0, -4.0, -6.0])


def pack_weight(w, fmt):
    k, n = w.shape
    w = f64(bf(w)).reshape(k // 32, 32, n)
    amax = np.abs(w).max(1)
    if fmt == "e4m3":
        byte = np.frexp(amax)[1] - 1 + 127 - 7
    else:
        mant, ex = np.frexp(amax / 6.0)
        byte = np.where(mant > 0.5, ex, ex - 1) + 127
    byte = np.clip(np.where(amax > 0, byte, 1), 1, 254)
    scaled = (w * np.exp2(127.0 - byte)[:, None, :]).reshape(k, n).astype(np.float32)
    by_word = np.ascontiguousarray(scaled.reshape(k // 512, 128, 4, n).transpose(0, 1, 3, 2))
    if fmt == "e4m3":
        words = by_word.astype(ml_dtypes.float8_e4m3fn).view(np.uint8)
    else:
        c = by_word.astype(ml_dtypes.float4_e2m1fn).view(np.uint8) & 0xF
        words = c[..., 0::2] | (c[..., 1::2] << 4)
    return np.ascontiguousarray(words), np.ascontiguousarray(byte.astype(np.uint8).reshape(k // 512, 16, n))


def unpack_weight(words, scales, fmt):
    g, p, n, _ = words.shape
    if fmt == "e4m3":
        vals = np.ascontiguousarray(words).view(ml_dtypes.float8_e4m3fn).astype(np.float64)
    else:
        nib = np.empty((g, p, n, 4), np.uint8)
        nib[..., 0::2] = words & 0xF
        nib[..., 1::2] = words >> 4
        vals = E2M1[nib]
    vals = vals * np.repeat(np.exp2(scales.astype(np.float64) - 127.0), 8, axis=1)[..., None]
    return vals.transpose(0, 1, 3, 2).reshape(g * 512, n)


B, N, M, F, D = 2, 1, 8, 2048, 2048
EPS = 1e-5
FMT = "e4m3"


def setup_inputs():
    s, t = mx_kscale(F), mx_kscale(F)
    s5 = np.tile(s, 5)
    x = bf(np.random.standard_normal((B, N, M, F)) * s)
    W1 = np.random.standard_normal((F, 5 * F)) * 0.7 / np.sqrt(F) / s5
    W1_words, W1_scales = pack_weight(np.ascontiguousarray(W1.T), FMT)
    b1 = bf(np.random.standard_normal(F) * 0.2)
    gamma = bf((1.0 + 0.1 * np.random.standard_normal(F)) * t)
    beta = bf(0.1 * np.random.standard_normal(F) * t)
    bias_p = bf(0.5 * np.random.standard_normal(F) * t)
    W2 = np.random.standard_normal((D, F)) / np.sqrt(F) / t
    W2_words, W2_scales = pack_weight(np.ascontiguousarray(W2.T), FMT)
    b2 = bf(np.random.standard_normal(D) * 0.3)
    return {
        "x": x,
        "W1_words": W1_words,
        "W1_scales": W1_scales,
        "b1": b1,
        "gamma": gamma,
        "beta": beta,
        "bias_p": bias_p,
        "W2_words": W2_words,
        "W2_scales": W2_scales,
        "b2": b2,
    }


def reference(x, W1_words, W1_scales, b1, gamma, beta, bias_p, W2_words, W2_scales, b2):
    x = f64(x)
    b, n, m, f = x.shape
    e = np.eye(m)[:, :, None]
    xi = x[:, :, :, None, :]
    xj = x[:, :, None, :, :]
    mean = np.mean(x, axis=2, keepdims=True)[:, :, :, None, :]
    shp = (b, n, m, m, f)
    xAll = np.concatenate([
        xi * e,
        np.broadcast_to(xi, shp),
        np.broadcast_to(xj, shp),
        np.broadcast_to(mean * e, shp),
        np.broadcast_to(mean, shp),
    ], axis=-1)
    h = (mxq(xAll, 4, "e4m3") @ unpack_weight(W1_words, W1_scales, FMT)) + f64(b1)
    mu = np.mean(h, axis=-1, keepdims=True)
    var = np.mean((h - mu) ** 2, axis=-1, keepdims=True)
    h = (h - mu) / np.sqrt(var + EPS) * f64(gamma) + f64(beta)
    h = np.maximum(h, 0.0)
    h = h + f64(bias_p) * e
    return (mxq(h, 4, "e4m3") @ unpack_weight(W2_words, W2_scales, FMT)) + f64(b2)

@@ -1,0 +1,346 @@
+from contextlib import ExitStack
+
+import concourse.mybir as mybir
+from concourse.masks import make_identity
+
+F32 = mybir.dt.float32
+BF16 = mybir.dt.bfloat16
+I32 = mybir.dt.int32
+U32 = mybir.dt.uint32
+U8 = mybir.dt.uint8
+FP8X4 = mybir.dt.float8_e4m3fn_x4
+ALU = mybir.AluOpType
+ACT = mybir.ActivationFunctionType
+
+P = 128
+F = 2048
+NB = 4
+CB = 512
+EPS = 1e-5
+RING = 14
+SCALES_ON_GPSIMD = False
+PART_ORDER = (1, 2, 4, 0, 3)
+
+FLOPS = 2 * 128 * (5 * F + F) * F
+
+
+def tile_hoe_1_2_module_w_kernel(
+    tc, x, W1_words, W1_scales, b1, gamma, beta, bias_p, W2_words, W2_scales, b2, out
+):
+    nc = tc.nc
+    with ExitStack() as ctx:
+        ctx.enter_context(tc.manual_schedule())
+        const = ctx.enter_context(tc.tile_pool(name="const", bufs=1))
+        ring = ctx.enter_context(tc.tile_pool(name="ring", bufs=RING))
+        stage = ctx.enter_context(tc.tile_pool(name="stage", bufs=3))
+        accp = ctx.enter_context(tc.psum_pool(name="accp", bufs=1))
+        auxp = ctx.enter_context(tc.psum_pool(name="auxp", bufs=1))
+
+        groups = [(s, g) for s in PART_ORDER for g in range(4)]
+        loads = []
+        for idx in range(18):
+            s, g = groups[idx]
+            loads.append(("big", W1_words[4 * s + g], None))
+        s, g = groups[18]
+        for nb in range(NB):
+            loads.append(("pair", W1_words[4 * s + g : 4 * s + g + 2], nb))
+        for g in range(3):
+            loads.append(("big", W2_words[g], None))
+        for nb in range(NB):
+            loads.append(("small", W2_words[3], nb))
+        tiles = []
+        state = {"next": 0, "big_out": 0}
+
+        def issue_loads():
+            while state["next"] < len(loads):
+                kind, src, nb = loads[state["next"]]
+                if kind == "pair":
+                    wt = const.tile(
+                        [P, 2, CB], U32, name="wp%d" % state["next"], align_bytes=64
+                    )
+                    nc.sync.dma_start(
+                        out=wt[:].bitcast(I32),
+                        in_=src.rearrange("a p n t -> p a (n t)").bitcast(I32)[
+                            :, :, nb * CB : (nb + 1) * CB
+                        ],
+                    )
+                    tiles.append(wt)
+                    state["next"] += 1
+                    continue
+                words = src.rearrange("p n t -> p (n t)").bitcast(I32)
+                if kind == "big":
+                    if state["big_out"] >= RING:
+                        return
+                    wt = ring.tile([P, F], U32, name="wt", tag="wt", align_bytes=64)
+                    nc.sync.dma_start(out=wt[:].bitcast(I32), in_=words)
+                    state["big_out"] += 1
+                else:
+                    wt = const.tile(
+                        [P, CB], U32, name="ws%d" % state["next"], align_bytes=64
+                    )
+                    nc.sync.dma_start(
+                        out=wt[:].bitcast(I32), in_=words[:, nb * CB : (nb + 1) * CB]
+                    )
+                tiles.append(wt)
+                state["next"] += 1
+                if state["next"] == 1:
+                    return
+
+        issue_loads()
+
+        planes = const.tile([P, 6, F], U8, name="planes", align_bytes=64)
+        xr = const.tile([P, CB], BF16, name="xr", align_bytes=64)
+        eps = const.tile([P, 1], F32, name="eps")
+        dmy = const.tile([P, 1], F32, name="dmy")
+        ident = const.tile([P, P], F32, name="ident")
+        br = const.tile([P, F], BF16, name="br")
+        sel = const.tile([P, 2, P], BF16, name="sel")
+        z0 = const.tile([P, F], BF16, name="z0", align_bytes=64)
+        z3 = const.tile([P, F], BF16, name="z3", align_bytes=64)
+        bd = const.tile([P, F], BF16, name="bd")
+
+        nc.vector.memset(xr[64:128, :].bitcast(F32), 0.0)
+        nc.vector.memset(eps[:], EPS)
+        for a in range(6):
+            nc.vector.memset(planes[:, a, :].bitcast(I32), 0)
+
+        nc.scalar.dma_start(
+            out=xr[0:64, :], in_=x.rearrange("b n i (g k) -> (b n i g) k", g=4)
+        )
+        for v, vec in enumerate((gamma, beta, bias_p)):
+            nc.scalar.dma_start(
+                out=xr[64 + 4 * v : 68 + 4 * v, :],
+                in_=vec.rearrange("(g k) -> g k", g=4),
+            )
+        nc.scalar.activation(out=dmy[:], in_=eps[:], func=ACT.Sqrt)
+
+        make_identity(nc, ident[:])
+        nc.gpsimd.memset(br[:].bitcast(F32), 0.0)
+        nc.gpsimd.memset(sel[:].rearrange("p a m -> p (a m)").bitcast(F32), 0.0)
+        nc.gpsimd.memset(sel[0:32, 0, :], 1.0)
+        nc.gpsimd.memset(sel[32:64, 1, :], 1.0)
+        nc.scalar.dma_start(out=br[0:1, :], in_=b1.rearrange("(o n) -> o n", o=1))
+        nc.scalar.dma_start(out=br[32:33, :], in_=b2.rearrange("(o n) -> o n", o=1))
+
+        for a in list(PART_ORDER) + [5]:
+            src = W2_scales if a == 5 else W1_scales[4 * a : 4 * a + 4]
+            for q in range(4):
+                if SCALES_ON_GPSIMD:
+                    nc.gpsimd.dma_start(
+                        out=planes[32 * q : 32 * q + 16, a, :].bitcast(F32),
+                        in_=src[:, 4 * q : 4 * q + 4, :].bitcast(F32),
+                    )
+                else:
+                    nc.sync.dma_start(
+                        out=planes[32 * q : 32 * q + 16, a, :].bitcast(I32),
+                        in_=src[:, 4 * q : 4 * q + 4, :].bitcast(I32),
+                    )
+
+        nc.gpsimd.memset(z0[:].bitcast(F32), 0.0)
+        nc.gpsimd.memset(z3[:].bitcast(F32), 0.0)
+        nc.gpsimd.memset(bd[:].bitcast(F32), 0.0)
+
+        issue_loads()
+
+        tp = auxp.tile([P, CB], F32, name="tp", tag="aux0")
+        xw = xr[:].bitcast(F32)
+        for u in range(2):
+            nc.tensor.transpose(tp[:, u * P : (u + 1) * P], xw[:, u : 256 : 2], ident[:])
+        tpv = tp[:, 0:256].rearrange("p (u c) -> p u c", u=2)
+        xb = const.tile([P, 4, 16, 4], BF16, name="xb")
+        pb = const.tile([P, 4, 4, 4], BF16, name="pb")
+        nc.vector.tensor_copy(
+            out=xb[:].bitcast(F32),
+            in_=tpv[:, :, 0:64].rearrange("p u (r g) -> p g r u", g=4),
+        )
+        nc.vector.tensor_copy(
+            out=pb[:].bitcast(F32),
+            in_=tpv[:, :, 64:80].rearrange("p u (v g) -> p g v u", g=4),
+        )
+
+        aw = const.tile([P, 5, CB], U32, name="aw", align_bytes=64)
+        asc = const.tile([P, 5, CB], U8, name="asc", align_bytes=64)
+
+        def quantise_part(s, src):
+            nc.vector.quantize_mx(
+                out=aw[:, s, :].bitcast(FP8X4), scales=asc[:, s, :], in_=src
+            )
+
+        st1 = stage.tile([P, F], BF16, name="st1", tag="st", align_bytes=64)
+        nc.vector.tensor_copy(
+            out=st1[:].rearrange("p (a j t) -> p a j t", j=8, t=4),
+            in_=xb[:].rearrange("p g r t -> p (g r) t").unsqueeze(2).to_broadcast([P, 64, 8, 4]),
+        )
+        msum = const.tile([P, 8, 4], F32, name="msum")
+        nc.vector.tensor_reduce(
+            out=msum[:],
+            in_=xb[:].rearrange("p g (b i) t -> p (g b) t i", b=2),
+            axis=mybir.AxisListType.X,
+            op=ALU.add,
+        )
+        st2 = stage.tile([P, F], BF16, name="st2", tag="st", align_bytes=64)
+        nc.vector.tensor_copy(
+            out=st2[:].rearrange("p (a i c) -> p a i c", i=8, c=32),
+            in_=xb[:].rearrange("p g (b j) t -> p (g b) (j t)", b=2).unsqueeze(2).to_broadcast([P, 8, 8, 32]),
+        )
+        quantise_part(1, st1[:])
+        mb = const.tile([P, 8, 4], BF16, name="mb")
+        nc.vector.tensor_scalar(
+            out=mb[:], in0=msum[:], scalar1=0.125, scalar2=None, op0=ALU.mult
+        )
+        st4 = stage.tile([P, F], BF16, name="st4", tag="st", align_bytes=64)
+        nc.vector.tensor_copy(
+            out=st4[:].rearrange("p (a m t) -> p a m t", m=64, t=4),
+            in_=mb[:].unsqueeze(2).to_broadcast([P, 8, 64, 4]),
+        )
+        quantise_part(2, st2[:])
+        prm = const.tile([P, 4, 4, 4], F32, name="prm")
+        nc.vector.tensor_copy(out=prm[:], in_=pb[:])
+        nc.vector.tensor_copy(
+            out=z0[:].rearrange("p (a m t) -> p a m t", m=64, t=4)[:, :, 0:64:9, :],
+            in_=xb[:].rearrange("p g (b i) t -> p (g b) i t", b=2),
+        )
+        quantise_part(4, st4[:])
+        nc.vector.tensor_copy(
+            out=z3[:].rearrange("p (a m t) -> p a m t", m=64, t=4)[:, :, 0:64:9, :],
+            in_=mb[:].unsqueeze(2).to_broadcast([P, 8, 8, 4]),
+        )
+        quantise_part(0, z0[:])
+        bd4 = bd[:].rearrange("p (g w t) -> p g w t", g=4, t=4)
+        for b in range(2):
+            nc.vector.tensor_copy(
+                out=bd4[:, :, 64 * b : 64 * b + 64 : 9, :],
+                in_=pb[:, :, 2, :].unsqueeze(2).to_broadcast([P, 4, 8, 4]),
+            )
+        quantise_part(3, z3[:])
+
+        b1p = const.tile([P, NB, 4, P], BF16, name="b1p")
+        b2b = const.tile([P, NB, CB], BF16, name="b2b")
+        def spread_bias(which):
+            for nb in range(NB):
+                bc = auxp.tile([P, CB], F32, name="bc", tag="aux%d" % nb)
+                nc.tensor.matmul(
+                    bc[:],
+                    lhsT=sel[:, which, :],
+                    rhs=br[:, nb * CB : (nb + 1) * CB],
+                    start=True,
+                    stop=True,
+                )
+                if which == 0:
+                    nc.scalar.copy(
+                        out=b1p[:, nb], in_=bc[:].rearrange("w (p t) -> w t p", t=4)
+                    )
+                else:
+                    nc.scalar.copy(out=b2b[:, nb, :], in_=bc[:])
+
+        acc = [accp.tile([P, CB], F32, name="acc%d" % nb, tag="acc%d" % nb) for nb in range(NB)]
+        hp = const.tile([P, NB, 4, P], F32, name="hp", tag="hp")
+        st6 = const.tile([P, NB, 6], F32, name="st6")
+
+        def first_pass(idx, nb, rhs):
+            s, g = groups[idx]
+            nc.tensor.matmul_mx(
+                out=acc[nb][:],
+                lhsT=aw[:, s, g * P : (g + 1) * P].bitcast(FP8X4),
+                lhsT_scale=asc[:, s, g * P : (g + 1) * P],
+                rhs=rhs.bitcast(FP8X4),
+                rhs_scale=planes[4 * g : P, s, nb * CB : (nb + 1) * CB],
+                start=(idx == 0),
+                stop=(idx == 19),
+            )
+
+        for idx in range(18):
+            for nb in range(NB):
+                first_pass(idx, nb, tiles[idx][:, nb * CB : (nb + 1) * CB])
+            state["big_out"] -= 1
+            issue_loads()
+            if idx == 3:
+                spread_bias(0)
+            if idx == 5:
+                spread_bias(1)
+        for nb in range(NB):
+            first_pass(18, nb, tiles[18 + nb][:, 0, :])
+            first_pass(19, nb, tiles[18 + nb][:, 1, :])
+            nc.vector.tensor_tensor(
+                out=hp[:, nb],
+                in0=acc[nb][:].rearrange("w (p t) -> w t p", t=4),
+                in1=b1p[:, nb],
+                op=ALU.add,
+            )
+            nc.vector.bn_stats(
+                out=st6[:, nb, :], in_=hp[:, nb].rearrange("w t p -> w (t p)")
+            )
+
+        mv = const.tile([P, 2], F32, name="mv")
+        std = const.tile([P, 1], F32, name="std")
+        rstd = const.tile([P, 1], F32, name="rstd")
+        nc.vector.bn_aggr(out=mv[:], in_=st6[:].rearrange("w a c -> w (a c)"))
+        nc.scalar.activation(out=std[:], in_=mv[:, 1:2], func=ACT.Sqrt, bias=eps[:], scale=1.0)
+        nc.vector.reciprocal(out=rstd[:], in_=std[:])
+
+        for nb in range(NB):
+            nc.vector.tensor_scalar(
+                out=hp[:, nb].rearrange("w t p -> w (t p)"),
+                in0=hp[:, nb].rearrange("w t p -> w (t p)"),
+                scalar1=mv[:, 0:1],
+                scalar2=rstd[:],
+                op0=ALU.subtract,
+                op1=ALU.mult,
+            )
+        tts = []
+        for g in range(4):
+            tt = auxp.tile([P, 4, P], F32, name="tt", tag="aux%d" % g)
+            for t in range(4):
+                nc.tensor.transpose(tt[:, t, :], hp[:, g, t, :], ident[:])
+            tts.append(tt)
+
+        ut = const.tile([P, 4, 4, P], F32, name="ut")
+        yg = const.tile([P, 4, P, 4], BF16, name="yg", align_bytes=64)
+        yw = const.tile([P, 4, P], U32, name="yw", align_bytes=64)
+        ys = const.tile([P, 4, P], U8, name="ys", align_bytes=64)
+        ot = const.tile([P, NB, CB], F32, name="ot", tag="hp")
+        acc2 = [accp.tile([P, CB], F32, name="out%d" % nb, tag="acc%d" % nb) for nb in range(NB)]
+        out_flat = out.rearrange("b n i j d -> (b n i j) d")
+        for g in range(4):
+            for t in range(4):
+                nc.scalar.activation(
+                    out=ut[:, g, t, :],
+                    in_=tts[g][:, t, :],
+                    func=ACT.Identity,
+                    scale=prm[:, g, 0, t : t + 1],
+                    bias=prm[:, g, 1, t : t + 1],
+                )
+            nc.vector.scalar_tensor_tensor(
+                out=yg[:, g],
+                in0=ut[:, g].rearrange("p t w -> p w t"),
+                scalar=0.0,
+                in1=bd4[:, g],
+                op0=ALU.max,
+                op1=ALU.add,
+            )
+            nc.vector.quantize_mx(
+                out=yw[:, g, :].bitcast(FP8X4),
+                scales=ys[:, g, :],
+                in_=yg[:, g].rearrange("p w t -> p (w t)"),
+            )
+            for nb in range(NB):
+                if g < 3:
+                    rhs = tiles[22 + g][:, nb * CB : (nb + 1) * CB]
+                else:
+                    rhs = tiles[25 + nb][:]
+                nc.tensor.matmul_mx(
+                    out=acc2[nb][:],
+                    lhsT=yw[:, g, :].bitcast(FP8X4),
+                    lhsT_scale=ys[:, g, :],
+                    rhs=rhs.bitcast(FP8X4),
+                    rhs_scale=planes[4 * g : P, 5, nb * CB : (nb + 1) * CB],
+                    start=(g == 0),
+                    stop=(g == 3),
+                )
+        for nb in range(NB):
+            nc.vector.tensor_tensor(
+                out=ot[:, nb, :], in0=acc2[nb][:], in1=b2b[:, nb, :], op=ALU.add
+            )
+            nc.sync.dma_start(
+                out=out_flat[:, nb * CB : (nb + 1) * CB], in_=ot[:, nb, :]
+            )

@@ -18,7 +18,7 @@ NB = 4
 CB = 512
 EPS = 1e-5
 RING = 14
-SCALES_ON_GPSIMD = False
+SCALES_ON_GPSIMD = True
 PART_ORDER = (1, 2, 4, 0, 3)
 
 FLOPS = 2 * 128 * (5 * F + F) * F
@@ -114,15 +114,7 @@ def tile_hoe_1_2_module_w_kernel(
             )
         nc.scalar.activation(out=dmy[:], in_=eps[:], func=ACT.Sqrt)
 
-        make_identity(nc, ident[:])
-        nc.gpsimd.memset(br[:].bitcast(F32), 0.0)
-        nc.gpsimd.memset(sel[:].rearrange("p a m -> p (a m)").bitcast(F32), 0.0)
-        nc.gpsimd.memset(sel[0:32, 0, :], 1.0)
-        nc.gpsimd.memset(sel[32:64, 1, :], 1.0)
-        nc.scalar.dma_start(out=br[0:1, :], in_=b1.rearrange("(o n) -> o n", o=1))
-        nc.scalar.dma_start(out=br[32:33, :], in_=b2.rearrange("(o n) -> o n", o=1))
-
-        for a in list(PART_ORDER) + [5]:
+        def load_planes(a):
             src = W2_scales if a == 5 else W1_scales[4 * a : 4 * a + 4]
             for q in range(4):
                 if SCALES_ON_GPSIMD:
@@ -136,9 +128,21 @@ def tile_hoe_1_2_module_w_kernel(
                         in_=src[:, 4 * q : 4 * q + 4, :].bitcast(I32),
                     )
 
+        make_identity(nc, ident[:])
+        load_planes(PART_ORDER[0])
+        load_planes(PART_ORDER[1])
+        nc.gpsimd.memset(br[:].bitcast(F32), 0.0)
+        nc.gpsimd.memset(sel[:].rearrange("p a m -> p (a m)").bitcast(F32), 0.0)
+        nc.gpsimd.memset(sel[0:32, 0, :], 1.0)
+        nc.gpsimd.memset(sel[32:64, 1, :], 1.0)
+        nc.scalar.dma_start(out=br[0:1, :], in_=b1.rearrange("(o n) -> o n", o=1))
+        nc.scalar.dma_start(out=br[32:33, :], in_=b2.rearrange("(o n) -> o n", o=1))
+
         nc.gpsimd.memset(z0[:].bitcast(F32), 0.0)
         nc.gpsimd.memset(z3[:].bitcast(F32), 0.0)
         nc.gpsimd.memset(bd[:].bitcast(F32), 0.0)
+        for a in list(PART_ORDER[2:]) + [5]:
+            load_planes(a)
 
         issue_loads()
 
@@ -254,9 +258,9 @@ def tile_hoe_1_2_module_w_kernel(
                 first_pass(idx, nb, tiles[idx][:, nb * CB : (nb + 1) * CB])
             state["big_out"] -= 1
             issue_loads()
-            if idx == 3:
+            if idx == 6:
                 spread_bias(0)
-            if idx == 5:
+            if idx == 8:
                 spread_bias(1)
         for nb in range(NB):
             first_pass(18, nb, tiles[18 + nb][:, 0, :])

@@ -20,6 +20,7 @@ EPS = 1e-5
 RING = 14
 SCALES_ON_GPSIMD = True
 PART_ORDER = (1, 2, 4, 0, 3)
+W2_ORDER = (3, 0, 1, 2)
 
 FLOPS = 2 * 128 * (5 * F + F) * F
 
@@ -44,10 +45,10 @@ def tile_hoe_1_2_module_w_kernel(
         s, g = groups[18]
         for nb in range(NB):
             loads.append(("pair", W1_words[4 * s + g : 4 * s + g + 2], nb))
-        for g in range(3):
+        for g in W2_ORDER[:3]:
             loads.append(("big", W2_words[g], None))
         for nb in range(NB):
-            loads.append(("small", W2_words[3], nb))
+            loads.append(("small", W2_words[W2_ORDER[3]], nb))
         tiles = []
         state = {"next": 0, "big_out": 0}
 
@@ -112,7 +113,7 @@ def tile_hoe_1_2_module_w_kernel(
                 out=xr[64 + 4 * v : 68 + 4 * v, :],
                 in_=vec.rearrange("(g k) -> g k", g=4),
             )
-        nc.scalar.activation(out=dmy[:], in_=eps[:], func=ACT.Sqrt)
+        nc.scalar.activation(out=dmy[:], in_=eps[:], func=ACT.Abs_reciprocal_sqrt)
 
         def load_planes(a):
             src = W2_scales if a == 5 else W1_scales[4 * a : 4 * a + 4]
@@ -276,27 +277,37 @@ def tile_hoe_1_2_module_w_kernel(
             )
 
         mv = const.tile([P, 2], F32, name="mv")
-        std = const.tile([P, 1], F32, name="std")
         rstd = const.tile([P, 1], F32, name="rstd")
+        nmr = const.tile([P, 1], F32, name="nmr")
         nc.vector.bn_aggr(out=mv[:], in_=st6[:].rearrange("w a c -> w (a c)"))
-        nc.scalar.activation(out=std[:], in_=mv[:, 1:2], func=ACT.Sqrt, bias=eps[:], scale=1.0)
-        nc.vector.reciprocal(out=rstd[:], in_=std[:])
+        nc.scalar.activation(
+            out=rstd[:], in_=mv[:, 1:2], func=ACT.Abs_reciprocal_sqrt, bias=eps[:], scale=1.0
+        )
+        nc.vector.tensor_scalar(
+            out=nmr[:], in0=mv[:, 0:1], scalar1=rstd[:], scalar2=-1.0, op0=ALU.mult, op1=ALU.mult
+        )
 
-        for nb in range(NB):
+        def flat(nb):
+            return hp[:, nb].rearrange("w t p -> w (t p)")
+
+        nc.scalar.activation(
+            out=flat(3), in_=flat(3), func=ACT.Identity, scale=rstd[:], bias=nmr[:]
+        )
+        for nb in range(3):
             nc.vector.tensor_scalar(
-                out=hp[:, nb].rearrange("w t p -> w (t p)"),
-                in0=hp[:, nb].rearrange("w t p -> w (t p)"),
+                out=flat(nb),
+                in0=flat(nb),
                 scalar1=mv[:, 0:1],
                 scalar2=rstd[:],
                 op0=ALU.subtract,
                 op1=ALU.mult,
             )
-        tts = []
-        for g in range(4):
+        tts = {}
+        for g in (0, 3, 1, 2):
             tt = auxp.tile([P, 4, P], F32, name="tt", tag="aux%d" % g)
             for t in range(4):
                 nc.tensor.transpose(tt[:, t, :], hp[:, g, t, :], ident[:])
-            tts.append(tt)
+            tts[g] = tt
 
         ut = const.tile([P, 4, 4, P], F32, name="ut")
         yg = const.tile([P, 4, P, 4], BF16, name="yg", align_bytes=64)
@@ -305,31 +316,52 @@ def tile_hoe_1_2_module_w_kernel(
         ot = const.tile([P, NB, CB], F32, name="ot", tag="hp")
         acc2 = [accp.tile([P, CB], F32, name="out%d" % nb, tag="acc%d" % nb) for nb in range(NB)]
         out_flat = out.rearrange("b n i j d -> (b n i j) d")
-        for g in range(4):
-            for t in range(4):
-                nc.scalar.activation(
-                    out=ut[:, g, t, :],
-                    in_=tts[g][:, t, :],
-                    func=ACT.Identity,
-                    scale=prm[:, g, 0, t : t + 1],
-                    bias=prm[:, g, 1, t : t + 1],
+        for pos, g in enumerate(W2_ORDER):
+            if g == 3:
+                for t in range(4):
+                    nc.vector.tensor_scalar(
+                        out=ut[:, g, t, :],
+                        in0=tts[g][:, t, :],
+                        scalar1=prm[:, g, 0, t : t + 1],
+                        scalar2=prm[:, g, 1, t : t + 1],
+                        op0=ALU.mult,
+                        op1=ALU.add,
+                    )
+                nc.vector.scalar_tensor_tensor(
+                    out=yg[:, g],
+                    in0=ut[:, g].rearrange("p t w -> p w t"),
+                    scalar=0.0,
+                    in1=bd4[:, g],
+                    op0=ALU.max,
+                    op1=ALU.add,
                 )
-            nc.vector.scalar_tensor_tensor(
-                out=yg[:, g],
-                in0=ut[:, g].rearrange("p t w -> p w t"),
-                scalar=0.0,
-                in1=bd4[:, g],
-                op0=ALU.max,
-                op1=ALU.add,
-            )
+            else:
+                for t in range(4):
+                    nc.scalar.activation(
+                        out=ut[:, g, t, :],
+                        in_=tts[g][:, t, :],
+                        func=ACT.Relu,
+                        scale=prm[:, g, 0, t : t + 1],
+                        bias=prm[:, g, 1, t : t + 1],
+                    )
+                diag = ut[:, g].rearrange("p t (b m) -> p t b m", b=2)[:, :, :, 0:64:9]
+                nc.vector.tensor_tensor(
+                    out=diag,
+                    in0=diag,
+                    in1=prm[:, g, 2, :].unsqueeze(2).unsqueeze(3).to_broadcast([P, 4, 2, 8]),
+                    op=ALU.add,
+                )
+                nc.vector.tensor_copy(
+                    out=yg[:, g], in_=ut[:, g].rearrange("p t w -> p w t")
+                )
             nc.vector.quantize_mx(
                 out=yw[:, g, :].bitcast(FP8X4),
                 scales=ys[:, g, :],
                 in_=yg[:, g].rearrange("p w t -> p (w t)"),
             )
             for nb in range(NB):
-                if g < 3:
-                    rhs = tiles[22 + g][:, nb * CB : (nb + 1) * CB]
+                if pos < 3:
+                    rhs = tiles[22 + pos][:, nb * CB : (nb + 1) * CB]
                 else:
                     rhs = tiles[25 + nb][:]
                 nc.tensor.matmul_mx(
@@ -338,8 +370,8 @@ def tile_hoe_1_2_module_w_kernel(
                     lhsT_scale=ys[:, g, :],
                     rhs=rhs.bitcast(FP8X4),
                     rhs_scale=planes[4 * g : P, 5, nb * CB : (nb + 1) * CB],
-                    start=(g == 0),
-                    stop=(g == 3),
+                    start=(pos == 0),
+                    stop=(pos == 3),
                 )
         for nb in range(NB):
             nc.vector.tensor_tensor(

@@ -20,7 +20,7 @@ EPS = 1e-5
 RING = 14
 SCALES_ON_GPSIMD = True
 PART_ORDER = (1, 2, 4, 0, 3)
-W2_ORDER = (3, 0, 1, 2)
+EARLY_AT = 14
 
 FLOPS = 2 * 128 * (5 * F + F) * F
 
@@ -45,10 +45,10 @@ def tile_hoe_1_2_module_w_kernel(
         s, g = groups[18]
         for nb in range(NB):
             loads.append(("pair", W1_words[4 * s + g : 4 * s + g + 2], nb))
-        for g in W2_ORDER[:3]:
+        for g in range(3):
             loads.append(("big", W2_words[g], None))
         for nb in range(NB):
-            loads.append(("small", W2_words[W2_ORDER[3]], nb))
+            loads.append(("small", W2_words[3], nb))
         tiles = []
         state = {"next": 0, "big_out": 0}
 
@@ -98,7 +98,6 @@ def tile_hoe_1_2_module_w_kernel(
         sel = const.tile([P, 2, P], BF16, name="sel")
         z0 = const.tile([P, F], BF16, name="z0", align_bytes=64)
         z3 = const.tile([P, F], BF16, name="z3", align_bytes=64)
-        bd = const.tile([P, F], BF16, name="bd")
 
         nc.vector.memset(xr[64:128, :].bitcast(F32), 0.0)
         nc.vector.memset(eps[:], EPS)
@@ -141,7 +140,6 @@ def tile_hoe_1_2_module_w_kernel(
 
         nc.gpsimd.memset(z0[:].bitcast(F32), 0.0)
         nc.gpsimd.memset(z3[:].bitcast(F32), 0.0)
-        nc.gpsimd.memset(bd[:].bitcast(F32), 0.0)
         for a in list(PART_ORDER[2:]) + [5]:
             load_planes(a)
 
@@ -211,12 +209,9 @@ def tile_hoe_1_2_module_w_kernel(
             in_=mb[:].unsqueeze(2).to_broadcast([P, 8, 8, 4]),
         )
         quantise_part(0, z0[:])
-        bd4 = bd[:].rearrange("p (g w t) -> p g w t", g=4, t=4)
-        for b in range(2):
-            nc.vector.tensor_copy(
-                out=bd4[:, :, 64 * b : 64 * b + 64 : 9, :],
-                in_=pb[:, :, 2, :].unsqueeze(2).to_broadcast([P, 4, 8, 4]),
-            )
+        nc.vector.tensor_tensor(
+            out=prm[:, :, 3, :], in0=prm[:, :, 1, :], in1=prm[:, :, 2, :], op=ALU.add
+        )
         quantise_part(3, z3[:])
 
         b1p = const.tile([P, NB, 4, P], BF16, name="b1p")
@@ -238,23 +233,53 @@ def tile_hoe_1_2_module_w_kernel(
                 else:
                     nc.scalar.copy(out=b2b[:, nb, :], in_=bc[:])
 
-        acc = [accp.tile([P, CB], F32, name="acc%d" % nb, tag="acc%d" % nb) for nb in range(NB)]
-        hp = const.tile([P, NB, 4, P], F32, name="hp", tag="hp")
-        st6 = const.tile([P, NB, 6], F32, name="st6")
+        acc_a = [accp.tile([P, CB], F32, name="acca%d" % nb, tag="acc%d" % nb) for nb in range(NB)]
+        acc_b = []
+        hp = const.tile([P, NB, 4, P], F32, name="hp")
+        zo = const.tile([P, NB, 4, P], F32, name="zo", tag="zo")
+        ub = const.tile([P, 4, 4, P], BF16, name="ub")
+        yg = const.tile([P, 4, P, 4], BF16, name="yg", align_bytes=64)
+        st6 = const.tile([P, 2, NB, 6], F32, name="st6")
+        mv = const.tile([P, 2, 2], F32, name="mv")
+        rstd_a = const.tile([P, 1], F32, name="rstd_a")
+        rstd_b = const.tile([P, 1], F32, name="rstd_b")
 
         def first_pass(idx, nb, rhs):
             s, g = groups[idx]
+            bank = acc_a[nb] if idx < 12 else acc_b[nb]
             nc.tensor.matmul_mx(
-                out=acc[nb][:],
+                out=bank[:],
                 lhsT=aw[:, s, g * P : (g + 1) * P].bitcast(FP8X4),
                 lhsT_scale=asc[:, s, g * P : (g + 1) * P],
                 rhs=rhs.bitcast(FP8X4),
                 rhs_scale=planes[4 * g : P, s, nb * CB : (nb + 1) * CB],
-                start=(idx == 0),
-                stop=(idx == 19),
+                start=(idx == 0 or idx == 12),
+                stop=(idx == 11 or idx == 19),
+            )
+
+        def flat(tile4, nb):
+            return tile4[:, nb].rearrange("w t p -> w (t p)")
+
+        def statistics(ph, rstd):
+            nc.vector.bn_aggr(out=mv[:, ph, :], in_=st6[:, ph].rearrange("w a c -> w (a c)"))
+            nc.scalar.activation(
+                out=rstd[:], in_=mv[:, ph, 1:2], func=ACT.Abs_reciprocal_sqrt, bias=eps[:], scale=1.0
+            )
+
+        def normalise(ph, rstd, dst, nb):
+            nc.vector.tensor_scalar(
+                out=flat(dst, nb),
+                in0=flat(hp, nb),
+                scalar1=mv[:, ph, 0:1],
+                scalar2=rstd[:],
+                op0=ALU.subtract,
+                op1=ALU.mult,
             )
 
         for idx in range(18):
+            if idx == 12:
+                for nb in range(NB):
+                    acc_b.append(auxp.tile([P, CB], F32, name="accb%d" % nb, tag="aux%d" % nb))
             for nb in range(NB):
                 first_pass(idx, nb, tiles[idx][:, nb * CB : (nb + 1) * CB])
             state["big_out"] -= 1
@@ -263,117 +288,104 @@ def tile_hoe_1_2_module_w_kernel(
                 spread_bias(0)
             if idx == 8:
                 spread_bias(1)
+            if idx == 11:
+                for nb in range(NB):
+                    nc.vector.tensor_tensor(
+                        out=hp[:, nb],
+                        in0=acc_a[nb][:].rearrange("w (p t) -> w t p", t=4),
+                        in1=b1p[:, nb],
+                        op=ALU.add,
+                    )
+                    nc.vector.bn_stats(out=st6[:, 0, nb, :], in_=flat(hp, nb))
+                statistics(0, rstd_a)
+                for nb in range(NB):
+                    normalise(0, rstd_a, zo, nb)
+            if idx == EARLY_AT:
+                for g in range(4):
+                    tt = accp.tile([P, 4, P], F32, name="tta", tag="acc%d" % g)
+                    for t in range(4):
+                        nc.tensor.transpose(tt[:, t, :], zo[:, g, t, :], ident[:])
+                    for t in range(4):
+                        nc.scalar.activation(
+                            out=ub[:, g, t, :],
+                            in_=tt[:, t, :],
+                            func=ACT.Relu,
+                            scale=prm[:, g, 0, t : t + 1],
+                            bias=prm[:, g, 1, t : t + 1],
+                        )
+                    nc.vector.tensor_copy(
+                        out=yg[:, g], in_=ub[:, g].rearrange("p t w -> p w t")
+                    )
         for nb in range(NB):
             first_pass(18, nb, tiles[18 + nb][:, 0, :])
             first_pass(19, nb, tiles[18 + nb][:, 1, :])
             nc.vector.tensor_tensor(
                 out=hp[:, nb],
-                in0=acc[nb][:].rearrange("w (p t) -> w t p", t=4),
-                in1=b1p[:, nb],
+                in0=acc_b[nb][:].rearrange("w (p t) -> w t p", t=4),
+                in1=hp[:, nb],
                 op=ALU.add,
             )
-            nc.vector.bn_stats(
-                out=st6[:, nb, :], in_=hp[:, nb].rearrange("w t p -> w (t p)")
-            )
-
-        mv = const.tile([P, 2], F32, name="mv")
-        rstd = const.tile([P, 1], F32, name="rstd")
-        nmr = const.tile([P, 1], F32, name="nmr")
-        nc.vector.bn_aggr(out=mv[:], in_=st6[:].rearrange("w a c -> w (a c)"))
-        nc.scalar.activation(
-            out=rstd[:], in_=mv[:, 1:2], func=ACT.Abs_reciprocal_sqrt, bias=eps[:], scale=1.0
-        )
-        nc.vector.tensor_scalar(
-            out=nmr[:], in0=mv[:, 0:1], scalar1=rstd[:], scalar2=-1.0, op0=ALU.mult, op1=ALU.mult
-        )
-
-        def flat(nb):
-            return hp[:, nb].rearrange("w t p -> w (t p)")
-
-        nc.scalar.activation(
-            out=flat(3), in_=flat(3), func=ACT.Identity, scale=rstd[:], bias=nmr[:]
-        )
-        for nb in range(3):
-            nc.vector.tensor_scalar(
-                out=flat(nb),
-                in0=flat(nb),
-                scalar1=mv[:, 0:1],
-                scalar2=rstd[:],
-                op0=ALU.subtract,
-                op1=ALU.mult,
-            )
-        tts = {}
-        for g in (0, 3, 1, 2):
-            tt = auxp.tile([P, 4, P], F32, name="tt", tag="aux%d" % g)
+            nc.vector.bn_stats(out=st6[:, 1, nb, :], in_=flat(hp, nb))
+        statistics(1, rstd_b)
+        for nb in range(NB):
+            normalise(1, rstd_b, hp, nb)
+        tts = []
+        for g in range(4):
+            tt = auxp.tile([P, 4, P], F32, name="ttb", tag="aux%d" % g)
             for t in range(4):
                 nc.tensor.transpose(tt[:, t, :], hp[:, g, t, :], ident[:])
-            tts[g] = tt
+            tts.append(tt)
 
-        ut = const.tile([P, 4, 4, P], F32, name="ut")
-        yg = const.tile([P, 4, P, 4], BF16, name="yg", align_bytes=64)
+        dt = const.tile([P, 4, 2, 8, 4], F32, name="dt")
         yw = const.tile([P, 4, P], U32, name="yw", align_bytes=64)
         ys = const.tile([P, 4, P], U8, name="ys", align_bytes=64)
-        ot = const.tile([P, NB, CB], F32, name="ot", tag="hp")
+        ot = const.tile([P, NB, CB], F32, name="ot", tag="zo")
         acc2 = [accp.tile([P, CB], F32, name="out%d" % nb, tag="acc%d" % nb) for nb in range(NB)]
         out_flat = out.rearrange("b n i j d -> (b n i j) d")
-        for pos, g in enumerate(W2_ORDER):
-            if g == 3:
-                for t in range(4):
-                    nc.vector.tensor_scalar(
-                        out=ut[:, g, t, :],
-                        in0=tts[g][:, t, :],
-                        scalar1=prm[:, g, 0, t : t + 1],
-                        scalar2=prm[:, g, 1, t : t + 1],
-                        op0=ALU.mult,
-                        op1=ALU.add,
-                    )
-                nc.vector.scalar_tensor_tensor(
-                    out=yg[:, g],
-                    in0=ut[:, g].rearrange("p t w -> p w t"),
-                    scalar=0.0,
-                    in1=bd4[:, g],
-                    op0=ALU.max,
-                    op1=ALU.add,
-                )
+
+        def spread(g, v):
+            return prm[:, g, v, :].unsqueeze(1).unsqueeze(1).to_broadcast([P, 2, 8, 4])
+
+        def second_pass(g, nb):
+            if g < 3:
+                rhs = tiles[22 + g][:, nb * CB : (nb + 1) * CB]
             else:
-                for t in range(4):
-                    nc.scalar.activation(
-                        out=ut[:, g, t, :],
-                        in_=tts[g][:, t, :],
-                        func=ACT.Relu,
-                        scale=prm[:, g, 0, t : t + 1],
-                        bias=prm[:, g, 1, t : t + 1],
-                    )
-                diag = ut[:, g].rearrange("p t (b m) -> p t b m", b=2)[:, :, :, 0:64:9]
-                nc.vector.tensor_tensor(
-                    out=diag,
-                    in0=diag,
-                    in1=prm[:, g, 2, :].unsqueeze(2).unsqueeze(3).to_broadcast([P, 4, 2, 8]),
-                    op=ALU.add,
-                )
-                nc.vector.tensor_copy(
-                    out=yg[:, g], in_=ut[:, g].rearrange("p t w -> p w t")
-                )
+                rhs = tiles[25 + nb][:]
+            nc.tensor.matmul_mx(
+                out=acc2[nb][:],
+                lhsT=yw[:, g, :].bitcast(FP8X4),
+                lhsT_scale=ys[:, g, :],
+                rhs=rhs.bitcast(FP8X4),
+                rhs_scale=planes[4 * g : P, 5, nb * CB : (nb + 1) * CB],
+                start=(g == 0),
+                stop=(g == 3),
+            )
+
+        for g in range(4):
+            nc.vector.tensor_tensor(
+                out=dt[:, g],
+                in0=tts[g][:].rearrange("p t (b m) -> p b m t", b=2)[:, :, 0:64:9, :],
+                in1=spread(g, 0),
+                op=ALU.mult,
+            )
+            nc.vector.tensor_tensor(out=dt[:, g], in0=dt[:, g], in1=spread(g, 3), op=ALU.add)
+            nc.vector.tensor_tensor(
+                out=yg[:, g].rearrange("p (b m) t -> p b m t", b=2)[:, :, 0:64:9, :],
+                in0=dt[:, g],
+                in1=spread(g, 2),
+                op=ALU.max,
+            )
             nc.vector.quantize_mx(
                 out=yw[:, g, :].bitcast(FP8X4),
                 scales=ys[:, g, :],
                 in_=yg[:, g].rearrange("p w t -> p (w t)"),
             )
-            for nb in range(NB):
-                if pos < 3:
-                    rhs = tiles[22 + pos][:, nb * CB : (nb + 1) * CB]
-                else:
-                    rhs = tiles[25 + nb][:]
-                nc.tensor.matmul_mx(
-                    out=acc2[nb][:],
-                    lhsT=yw[:, g, :].bitcast(FP8X4),
-                    lhsT_scale=ys[:, g, :],
-                    rhs=rhs.bitcast(FP8X4),
-                    rhs_scale=planes[4 * g : P, 5, nb * CB : (nb + 1) * CB],
-                    start=(pos == 0),
-                    stop=(pos == 3),
-                )
+            if g < 2:
+                for nb in range(NB):
+                    second_pass(g, nb)
         for nb in range(NB):
+            second_pass(2, nb)
+            second_pass(3, nb)
             nc.vector.tensor_tensor(
                 out=ot[:, nb, :], in0=acc2[nb][:], in1=b2b[:, nb, :], op=ALU.add
             )

@@ -21,6 +21,7 @@ RING = 14
 SCALES_ON_GPSIMD = True
 PART_ORDER = (1, 2, 4, 0, 3)
 EARLY_AT = 14
+WARM = (3, 1, 5)
 
 FLOPS = 2 * 128 * (5 * F + F) * F
 
@@ -316,6 +317,24 @@ def tile_hoe_1_2_module_w_kernel(
                     nc.vector.tensor_copy(
                         out=yg[:, g], in_=ub[:, g].rearrange("p t w -> p w t")
                     )
+        hd = const.tile([P, 4, 2, 8, 4], F32, name="hd")
+        dt = const.tile([P, 4, 2, 8, 4], F32, name="dt")
+        yw = const.tile([P, 4, P], U32, name="yw", align_bytes=64)
+        ys = const.tile([P, 4, P], U8, name="ys", align_bytes=64)
+
+        def raw_transposes(g):
+            tt = auxp.tile([P, 4, P], F32, name="ttb", tag="aux%d" % g)
+            for t in range(4):
+                nc.tensor.transpose(tt[:, t, :], hp[:, g, t, :], ident[:])
+            src = tt[:].rearrange("p t (b m) -> p b m t", b=2)[:, :, 0:64:9, :]
+            if g < 3:
+                nc.scalar.copy(out=hd[:, g], in_=src)
+            else:
+                nc.vector.tensor_copy(out=hd[:, g], in_=src)
+
+        def late_stats(nb):
+            nc.vector.bn_stats(out=st6[:, 1, nb, :], in_=flat(hp, nb))
+
         for nb in range(NB):
             first_pass(18, nb, tiles[18 + nb][:, 0, :])
             first_pass(19, nb, tiles[18 + nb][:, 1, :])
@@ -325,26 +344,47 @@ def tile_hoe_1_2_module_w_kernel(
                 in1=hp[:, nb],
                 op=ALU.add,
             )
-            nc.vector.bn_stats(out=st6[:, 1, nb, :], in_=flat(hp, nb))
-        statistics(1, rstd_b)
-        for nb in range(NB):
-            normalise(1, rstd_b, hp, nb)
-        tts = []
-        for g in range(4):
-            tt = auxp.tile([P, 4, P], F32, name="ttb", tag="aux%d" % g)
-            for t in range(4):
-                nc.tensor.transpose(tt[:, t, :], hp[:, g, t, :], ident[:])
-            tts.append(tt)
+            if nb == 0:
+                late_stats(0)
+            if nb >= 2:
+                late_stats(nb - 1)
+            if nb >= 1:
+                raw_transposes(nb - 1)
+        late_stats(3)
+        raw_transposes(3)
+        wm = accp.tile([P, CB], F32, name="wm", tag="acc3")
 
-        dt = const.tile([P, 4, 2, 8, 4], F32, name="dt")
-        yw = const.tile([P, 4, P], U32, name="yw", align_bytes=64)
-        ys = const.tile([P, 4, P], U8, name="ys", align_bytes=64)
+        def keep_warm(count):
+            for i in range(count):
+                nc.tensor.matmul(
+                    wm[:], lhsT=sel[:, 0, :], rhs=br[:, 0:CB], start=True, stop=True
+                )
+
+        keep_warm(WARM[0])
+        nc.vector.bn_aggr(out=mv[:, 1, :], in_=st6[:, 1].rearrange("w a c -> w (a c)"))
+        nc.scalar.activation(
+            out=rstd_b[:], in_=mv[:, 1, 1:2], func=ACT.Abs_reciprocal_sqrt, bias=eps[:], scale=1.0
+        )
+        tm = auxp.tile([P, P], F32, name="tm", tag="aux0")
+        nc.tensor.transpose(tm[:], mv[:, 1, 0:1].to_broadcast([P, P]), ident[:])
+        keep_warm(WARM[1])
+        tr = auxp.tile([P, P], F32, name="tr", tag="aux1")
+        nc.tensor.transpose(tr[:], rstd_b[:, 0:1].to_broadcast([P, P]), ident[:])
+        keep_warm(WARM[2])
+
         ot = const.tile([P, NB, CB], F32, name="ot", tag="zo")
         acc2 = [accp.tile([P, CB], F32, name="out%d" % nb, tag="acc%d" % nb) for nb in range(NB)]
         out_flat = out.rearrange("b n i j d -> (b n i j) d")
 
         def spread(g, v):
             return prm[:, g, v, :].unsqueeze(1).unsqueeze(1).to_broadcast([P, 2, 8, 4])
+
+        def of_rows(ps):
+            return (
+                ps[:].rearrange("p (b m) -> p b m", b=2)[:, :, 0:64:9]
+                .unsqueeze(3)
+                .to_broadcast([P, 2, 8, 4])
+            )
 
         def second_pass(g, nb):
             if g < 3:
@@ -362,30 +402,29 @@ def tile_hoe_1_2_module_w_kernel(
             )
 
         for g in range(4):
-            nc.vector.tensor_tensor(
-                out=dt[:, g],
-                in0=tts[g][:].rearrange("p t (b m) -> p b m t", b=2)[:, :, 0:64:9, :],
-                in1=spread(g, 0),
-                op=ALU.mult,
-            )
+            nc.vector.tensor_tensor(out=hd[:, g], in0=hd[:, g], in1=of_rows(tm), op=ALU.subtract)
+        for g in range(4):
+            nc.vector.tensor_tensor(out=hd[:, g], in0=hd[:, g], in1=spread(g, 0), op=ALU.mult)
+        for g in range(4):
+            nc.vector.tensor_tensor(out=dt[:, g], in0=hd[:, g], in1=of_rows(tr), op=ALU.mult)
+        for g in range(4):
             nc.vector.tensor_tensor(out=dt[:, g], in0=dt[:, g], in1=spread(g, 3), op=ALU.add)
+        for g in range(4):
             nc.vector.tensor_tensor(
                 out=yg[:, g].rearrange("p (b m) t -> p b m t", b=2)[:, :, 0:64:9, :],
                 in0=dt[:, g],
                 in1=spread(g, 2),
                 op=ALU.max,
             )
+        for g in range(4):
             nc.vector.quantize_mx(
                 out=yw[:, g, :].bitcast(FP8X4),
                 scales=ys[:, g, :],
                 in_=yg[:, g].rearrange("p w t -> p (w t)"),
             )
-            if g < 2:
-                for nb in range(NB):
-                    second_pass(g, nb)
         for nb in range(NB):
-            second_pass(2, nb)
-            second_pass(3, nb)
+            for g in range(4):
+                second_pass(g, nb)
             nc.vector.tensor_tensor(
                 out=ot[:, nb, :], in0=acc2[nb][:], in1=b2b[:, nb, :], op=ALU.add
             )

@@ -21,7 +21,7 @@ RING = 14
 SCALES_ON_GPSIMD = True
 PART_ORDER = (1, 2, 4, 0, 3)
 EARLY_AT = 14
-WARM = (3, 1, 5)
+WARM = (0, 3, 5)
 
 FLOPS = 2 * 128 * (5 * F + F) * F
 
@@ -332,25 +332,42 @@ def tile_hoe_1_2_module_w_kernel(
             else:
                 nc.vector.tensor_copy(out=hd[:, g], in_=src)
 
-        def late_stats(nb):
-            nc.vector.bn_stats(out=st6[:, 1, nb, :], in_=flat(hp, nb))
-
+        ssum = const.tile([P, NB], F32, name="ssum")
+        qsum = const.tile([P, NB], F32, name="qsum")
+        sq = const.tile([P, CB], BF16, name="sq")
+        scr = const.tile([P, 2, NB], F32, name="scr")
+        mu_b = const.tile([P, 1], F32, name="mu_b")
+        ex2 = const.tile([P, 1], F32, name="ex2")
+        nvar = const.tile([P, 1], F32, name="nvar")
         for nb in range(NB):
             first_pass(18, nb, tiles[18 + nb][:, 0, :])
             first_pass(19, nb, tiles[18 + nb][:, 1, :])
-            nc.vector.tensor_tensor(
+            nc.vector.scalar_tensor_tensor(
                 out=hp[:, nb],
                 in0=acc_b[nb][:].rearrange("w (p t) -> w t p", t=4),
+                scalar=mv[:, 0, 0:1],
                 in1=hp[:, nb],
-                op=ALU.add,
+                op0=ALU.subtract,
+                op1=ALU.add,
+                accum_out=ssum[:, nb : nb + 1],
             )
-            if nb == 0:
-                late_stats(0)
-            if nb >= 2:
-                late_stats(nb - 1)
+            nc.scalar.activation(
+                out=sq[:], in_=flat(hp, nb), func=ACT.Square, accum_out=qsum[:, nb : nb + 1]
+            )
             if nb >= 1:
                 raw_transposes(nb - 1)
-        late_stats(3)
+        nc.vector.tensor_scalar(
+            out=scr[:, 0, 0:3], in0=qsum[:, 0:3], scalar1=1.0 / F, scalar2=EPS,
+            op0=ALU.mult, op1=ALU.add, accum_out=ex2[:],
+        )
+        nc.vector.tensor_scalar(
+            out=scr[:, 1, :], in0=ssum[:], scalar1=1.0 / F, scalar2=0.0,
+            op0=ALU.mult, op1=ALU.add, accum_out=mu_b[:],
+        )
+        nc.vector.tensor_scalar(
+            out=nvar[:], in0=mu_b[:], scalar1=mu_b[:], scalar2=ex2[:],
+            op0=ALU.mult, op1=ALU.subtract,
+        )
         raw_transposes(3)
         wm = accp.tile([P, CB], F32, name="wm", tag="acc3")
 
@@ -361,12 +378,11 @@ def tile_hoe_1_2_module_w_kernel(
                 )
 
         keep_warm(WARM[0])
-        nc.vector.bn_aggr(out=mv[:, 1, :], in_=st6[:, 1].rearrange("w a c -> w (a c)"))
         nc.scalar.activation(
-            out=rstd_b[:], in_=mv[:, 1, 1:2], func=ACT.Abs_reciprocal_sqrt, bias=eps[:], scale=1.0
+            out=rstd_b[:], in_=qsum[:, 3:4], func=ACT.Abs_reciprocal_sqrt, bias=nvar[:], scale=-1.0 / F
         )
         tm = auxp.tile([P, P], F32, name="tm", tag="aux0")
-        nc.tensor.transpose(tm[:], mv[:, 1, 0:1].to_broadcast([P, P]), ident[:])
+        nc.tensor.transpose(tm[:], mu_b[:, 0:1].to_broadcast([P, P]), ident[:])
         keep_warm(WARM[1])
         tr = auxp.tile([P, P], F32, name="tr", tag="aux1")
         nc.tensor.transpose(tr[:], rstd_b[:, 0:1].to_broadcast([P, P]), ident[:])
@@ -425,9 +441,14 @@ def tile_hoe_1_2_module_w_kernel(
         for nb in range(NB):
             for g in range(4):
                 second_pass(g, nb)
-            nc.vector.tensor_tensor(
-                out=ot[:, nb, :], in0=acc2[nb][:], in1=b2b[:, nb, :], op=ALU.add
-            )
-            nc.sync.dma_start(
-                out=out_flat[:, nb * CB : (nb + 1) * CB], in_=ot[:, nb, :]
-            )
+            pieces = 2 if nb == NB - 1 else 1
+            width = CB // pieces
+            for h in range(pieces):
+                cols = slice(h * width, (h + 1) * width)
+                nc.vector.tensor_tensor(
+                    out=ot[:, nb, cols], in0=acc2[nb][:, cols], in1=b2b[:, nb, cols], op=ALU.add
+                )
+                nc.sync.dma_start(
+                    out=out_flat[:, nb * CB + h * width : nb * CB + (h + 1) * width],
+                    in_=ot[:, nb, cols],
+                )

@@ -18,7 +18,6 @@ NB = 4
 CB = 512
 EPS = 1e-5
 RING = 14
-SCALES_ON_GPSIMD = True
 PART_ORDER = (1, 2, 4, 0, 3)
 EARLY_AT = 14
 WARM = (0, 3, 5)
@@ -102,7 +101,8 @@ def tile_hoe_1_2_module_w_kernel(
 
         nc.vector.memset(xr[64:128, :].bitcast(F32), 0.0)
         nc.vector.memset(eps[:], EPS)
-        for a in range(6):
+        nc.vector.memset(br[:].bitcast(F32), 0.0)
+        for a in list(PART_ORDER) + [5]:
             nc.vector.memset(planes[:, a, :].bitcast(I32), 0)
 
         nc.scalar.dma_start(
@@ -113,36 +113,29 @@ def tile_hoe_1_2_module_w_kernel(
                 out=xr[64 + 4 * v : 68 + 4 * v, :],
                 in_=vec.rearrange("(g k) -> g k", g=4),
             )
+        nc.scalar.dma_start(out=br[0:1, :], in_=b1.rearrange("(o n) -> o n", o=1))
+        nc.scalar.dma_start(out=br[32:33, :], in_=b2.rearrange("(o n) -> o n", o=1))
         nc.scalar.activation(out=dmy[:], in_=eps[:], func=ACT.Abs_reciprocal_sqrt)
 
-        def load_planes(a):
+        def load_planes(a, queue):
             src = W2_scales if a == 5 else W1_scales[4 * a : 4 * a + 4]
             for q in range(4):
-                if SCALES_ON_GPSIMD:
-                    nc.gpsimd.dma_start(
-                        out=planes[32 * q : 32 * q + 16, a, :].bitcast(F32),
-                        in_=src[:, 4 * q : 4 * q + 4, :].bitcast(F32),
-                    )
-                else:
-                    nc.sync.dma_start(
-                        out=planes[32 * q : 32 * q + 16, a, :].bitcast(I32),
-                        in_=src[:, 4 * q : 4 * q + 4, :].bitcast(I32),
-                    )
+                queue.dma_start(
+                    out=planes[32 * q : 32 * q + 16, a, :].bitcast(F32),
+                    in_=src[:, 4 * q : 4 * q + 4, :].bitcast(F32),
+                )
 
         make_identity(nc, ident[:])
-        load_planes(PART_ORDER[0])
-        load_planes(PART_ORDER[1])
-        nc.gpsimd.memset(br[:].bitcast(F32), 0.0)
+        load_planes(PART_ORDER[0], nc.scalar)
+        load_planes(PART_ORDER[1], nc.scalar)
         nc.gpsimd.memset(sel[:].rearrange("p a m -> p (a m)").bitcast(F32), 0.0)
         nc.gpsimd.memset(sel[0:32, 0, :], 1.0)
         nc.gpsimd.memset(sel[32:64, 1, :], 1.0)
-        nc.scalar.dma_start(out=br[0:1, :], in_=b1.rearrange("(o n) -> o n", o=1))
-        nc.scalar.dma_start(out=br[32:33, :], in_=b2.rearrange("(o n) -> o n", o=1))
 
         nc.gpsimd.memset(z0[:].bitcast(F32), 0.0)
         nc.gpsimd.memset(z3[:].bitcast(F32), 0.0)
         for a in list(PART_ORDER[2:]) + [5]:
-            load_planes(a)
+            load_planes(a, nc.gpsimd)
 
         issue_loads()
 

@@ -431,9 +431,11 @@ def tile_hoe_1_2_module_w_kernel(
                 scales=ys[:, g, :],
                 in_=yg[:, g].rearrange("p w t -> p (w t)"),
             )
-        for nb in range(NB):
-            for g in range(4):
+        for g in range(3):
+            for nb in range(NB):
                 second_pass(g, nb)
+        for nb in range(NB):
+            second_pass(3, nb)
             pieces = 2 if nb == NB - 1 else 1
             width = CB // pieces
             for h in range(pieces):

@@ -104,6 +104,11 @@ def tile_hoe_1_2_module_w_kernel(
         nc.vector.memset(br[:].bitcast(F32), 0.0)
         for a in list(PART_ORDER) + [5]:
             nc.vector.memset(planes[:, a, :].bitcast(I32), 0)
+        nc.vector.memset(sel[:].rearrange("p a m -> p (a m)").bitcast(F32), 0.0)
+        nc.vector.memset(sel[0:32, 0, :], 1.0)
+        nc.vector.memset(sel[32:64, 1, :], 1.0)
+        nc.vector.memset(z0[:].bitcast(F32), 0.0)
+        nc.vector.memset(z3[:].bitcast(F32), 0.0)
 
         nc.scalar.dma_start(
             out=xr[0:64, :], in_=x.rearrange("b n i (g k) -> (b n i g) k", g=4)
@@ -126,15 +131,7 @@ def tile_hoe_1_2_module_w_kernel(
                 )
 
         make_identity(nc, ident[:])
-        load_planes(PART_ORDER[0], nc.scalar)
-        load_planes(PART_ORDER[1], nc.scalar)
-        nc.gpsimd.memset(sel[:].rearrange("p a m -> p (a m)").bitcast(F32), 0.0)
-        nc.gpsimd.memset(sel[0:32, 0, :], 1.0)
-        nc.gpsimd.memset(sel[32:64, 1, :], 1.0)
-
-        nc.gpsimd.memset(z0[:].bitcast(F32), 0.0)
-        nc.gpsimd.memset(z3[:].bitcast(F32), 0.0)
-        for a in list(PART_ORDER[2:]) + [5]:
+        for a in list(PART_ORDER) + [5]:
             load_planes(a, nc.gpsimd)
 
         issue_loads()

from contextlib import ExitStack

import concourse.mybir as mybir
from concourse.masks import make_identity

F32 = mybir.dt.float32
BF16 = mybir.dt.bfloat16
I32 = mybir.dt.int32
U32 = mybir.dt.uint32
U8 = mybir.dt.uint8
FP8X4 = mybir.dt.float8_e4m3fn_x4
ALU = mybir.AluOpType
ACT = mybir.ActivationFunctionType

P = 128
F = 2048
NB = 4
CB = 512
EPS = 1e-5
RING = 14
PART_ORDER = (1, 2, 4, 0, 3)
EARLY_AT = 14
WARM = (0, 3, 5)

FLOPS = 2 * 128 * (5 * F + F) * F


def tile_hoe_1_2_module_w_kernel(
    tc, x, W1_words, W1_scales, b1, gamma, beta, bias_p, W2_words, W2_scales, b2, out
):
    nc = tc.nc
    with ExitStack() as ctx:
        ctx.enter_context(tc.manual_schedule())
        const = ctx.enter_context(tc.tile_pool(name="const", bufs=1))
        ring = ctx.enter_context(tc.tile_pool(name="ring", bufs=RING))
        stage = ctx.enter_context(tc.tile_pool(name="stage", bufs=3))
        accp = ctx.enter_context(tc.psum_pool(name="accp", bufs=1))
        auxp = ctx.enter_context(tc.psum_pool(name="auxp", bufs=1))

        groups = [(s, g) for s in PART_ORDER for g in range(4)]
        loads = []
        for idx in range(18):
            s, g = groups[idx]
            loads.append(("big", W1_words[4 * s + g], None))
        s, g = groups[18]
        for nb in range(NB):
            loads.append(("pair", W1_words[4 * s + g : 4 * s + g + 2], nb))
        for g in range(3):
            loads.append(("big", W2_words[g], None))
        for nb in range(NB):
            loads.append(("small", W2_words[3], nb))
        tiles = []
        state = {"next": 0, "big_out": 0}

        def issue_loads():
            while state["next"] < len(loads):
                kind, src, nb = loads[state["next"]]
                if kind == "pair":
                    wt = const.tile(
                        [P, 2, CB], U32, name="wp%d" % state["next"], align_bytes=64
                    )
                    nc.sync.dma_start(
                        out=wt[:].bitcast(I32),
                        in_=src.rearrange("a p n t -> p a (n t)").bitcast(I32)[
                            :, :, nb * CB : (nb + 1) * CB
                        ],
                    )
                    tiles.append(wt)
                    state["next"] += 1
                    continue
                words = src.rearrange("p n t -> p (n t)").bitcast(I32)
                if kind == "big":
                    if state["big_out"] >= RING:
                        return
                    wt = ring.tile([P, F], U32, name="wt", tag="wt", align_bytes=64)
                    nc.sync.dma_start(out=wt[:].bitcast(I32), in_=words)
                    state["big_out"] += 1
                else:
                    wt = const.tile(
                        [P, CB], U32, name="ws%d" % state["next"], align_bytes=64
                    )
                    nc.sync.dma_start(
                        out=wt[:].bitcast(I32), in_=words[:, nb * CB : (nb + 1) * CB]
                    )
                tiles.append(wt)
                state["next"] += 1
                if state["next"] == 1:
                    return

        issue_loads()

        planes = const.tile([P, 6, F], U8, name="planes", align_bytes=64)
        xr = const.tile([P, CB], BF16, name="xr", align_bytes=64)
        eps = const.tile([P, 1], F32, name="eps")
        dmy = const.tile([P, 1], F32, name="dmy")
        ident = const.tile([P, P], F32, name="ident")
        br = const.tile([P, F], BF16, name="br")
        sel = const.tile([P, 2, P], BF16, name="sel")
        z0 = const.tile([P, F], BF16, name="z0", align_bytes=64)
        z3 = const.tile([P, F], BF16, name="z3", align_bytes=64)

        nc.vector.memset(xr[64:128, :].bitcast(F32), 0.0)
        nc.vector.memset(eps[:], EPS)
        nc.vector.memset(br[:].bitcast(F32), 0.0)
        for a in list(PART_ORDER) + [5]:
            nc.vector.memset(planes[:, a, :].bitcast(I32), 0)
        nc.vector.memset(sel[:].rearrange("p a m -> p (a m)").bitcast(F32), 0.0)
        nc.vector.memset(sel[0:32, 0, :], 1.0)
        nc.vector.memset(sel[32:64, 1, :], 1.0)
        nc.vector.memset(z0[:].bitcast(F32), 0.0)
        nc.vector.memset(z3[:].bitcast(F32), 0.0)

        nc.scalar.dma_start(
            out=xr[0:64, :], in_=x.rearrange("b n i (g k) -> (b n i g) k", g=4)
        )
        for v, vec in enumerate((gamma, beta, bias_p)):
            nc.scalar.dma_start(
                out=xr[64 + 4 * v : 68 + 4 * v, :],
                in_=vec.rearrange("(g k) -> g k", g=4),
            )
        nc.scalar.dma_start(out=br[0:1, :], in_=b1.rearrange("(o n) -> o n", o=1))
        nc.scalar.dma_start(out=br[32:33, :], in_=b2.rearrange("(o n) -> o n", o=1))
        nc.scalar.activation(out=dmy[:], in_=eps[:], func=ACT.Abs_reciprocal_sqrt)

        def load_planes(a, queue):
            src = W2_scales if a == 5 else W1_scales[4 * a : 4 * a + 4]
            for q in range(4):
                queue.dma_start(
                    out=planes[32 * q : 32 * q + 16, a, :].bitcast(F32),
                    in_=src[:, 4 * q : 4 * q + 4, :].bitcast(F32),
                )

        make_identity(nc, ident[:])
        for a in list(PART_ORDER) + [5]:
            load_planes(a, nc.gpsimd)

        issue_loads()

        tp = auxp.tile([P, CB], F32, name="tp", tag="aux0")
        xw = xr[:].bitcast(F32)
        for u in range(2):
            nc.tensor.transpose(tp[:, u * P : (u + 1) * P], xw[:, u : 256 : 2], ident[:])
        tpv = tp[:, 0:256].rearrange("p (u c) -> p u c", u=2)
        xb = const.tile([P, 4, 16, 4], BF16, name="xb")
        pb = const.tile([P, 4, 4, 4], BF16, name="pb")
        nc.vector.tensor_copy(
            out=xb[:].bitcast(F32),
            in_=tpv[:, :, 0:64].rearrange("p u (r g) -> p g r u", g=4),
        )
        nc.vector.tensor_copy(
            out=pb[:].bitcast(F32),
            in_=tpv[:, :, 64:80].rearrange("p u (v g) -> p g v u", g=4),
        )

        aw = const.tile([P, 5, CB], U32, name="aw", align_bytes=64)
        asc = const.tile([P, 5, CB], U8, name="asc", align_bytes=64)

        def quantise_part(s, src):
            nc.vector.quantize_mx(
                out=aw[:, s, :].bitcast(FP8X4), scales=asc[:, s, :], in_=src
            )

        st1 = stage.tile([P, F], BF16, name="st1", tag="st", align_bytes=64)
        nc.vector.tensor_copy(
            out=st1[:].rearrange("p (a j t) -> p a j t", j=8, t=4),
            in_=xb[:].rearrange("p g r t -> p (g r) t").unsqueeze(2).to_broadcast([P, 64, 8, 4]),
        )
        msum = const.tile([P, 8, 4], F32, name="msum")
        nc.vector.tensor_reduce(
            out=msum[:],
            in_=xb[:].rearrange("p g (b i) t -> p (g b) t i", b=2),
            axis=mybir.AxisListType.X,
            op=ALU.add,
        )
        st2 = stage.tile([P, F], BF16, name="st2", tag="st", align_bytes=64)
        nc.vector.tensor_copy(
            out=st2[:].rearrange("p (a i c) -> p a i c", i=8, c=32),
            in_=xb[:].rearrange("p g (b j) t -> p (g b) (j t)", b=2).unsqueeze(2).to_broadcast([P, 8, 8, 32]),
        )
        quantise_part(1, st1[:])
        mb = const.tile([P, 8, 4], BF16, name="mb")
        nc.vector.tensor_scalar(
            out=mb[:], in0=msum[:], scalar1=0.125, scalar2=None, op0=ALU.mult
        )
        st4 = stage.tile([P, F], BF16, name="st4", tag="st", align_bytes=64)
        nc.vector.tensor_copy(
            out=st4[:].rearrange("p (a m t) -> p a m t", m=64, t=4),
            in_=mb[:].unsqueeze(2).to_broadcast([P, 8, 64, 4]),
        )
        quantise_part(2, st2[:])
        prm = const.tile([P, 4, 4, 4], F32, name="prm")
        nc.vector.tensor_copy(out=prm[:], in_=pb[:])
        nc.vector.tensor_copy(
            out=z0[:].rearrange("p (a m t) -> p a m t", m=64, t=4)[:, :, 0:64:9, :],
            in_=xb[:].rearrange("p g (b i) t -> p (g b) i t", b=2),
        )
        quantise_part(4, st4[:])
        nc.vector.tensor_copy(
            out=z3[:].rearrange("p (a m t) -> p a m t", m=64, t=4)[:, :, 0:64:9, :],
            in_=mb[:].unsqueeze(2).to_broadcast([P, 8, 8, 4]),
        )
        quantise_part(0, z0[:])
        nc.vector.tensor_tensor(
            out=prm[:, :, 3, :], in0=prm[:, :, 1, :], in1=prm[:, :, 2, :], op=ALU.add
        )
        quantise_part(3, z3[:])

        b1p = const.tile([P, NB, 4, P], BF16, name="b1p")
        b2b = const.tile([P, NB, CB], BF16, name="b2b")
        def spread_bias(which):
            for nb in range(NB):
                bc = auxp.tile([P, CB], F32, name="bc", tag="aux%d" % nb)
                nc.tensor.matmul(
                    bc[:],
                    lhsT=sel[:, which, :],
                    rhs=br[:, nb * CB : (nb + 1) * CB],
                    start=True,
                    stop=True,
                )
                if which == 0:
                    nc.scalar.copy(
                        out=b1p[:, nb], in_=bc[:].rearrange("w (p t) -> w t p", t=4)
                    )
                else:
                    nc.scalar.copy(out=b2b[:, nb, :], in_=bc[:])

        acc_a = [accp.tile([P, CB], F32, name="acca%d" % nb, tag="acc%d" % nb) for nb in range(NB)]
        acc_b = []
        hp = const.tile([P, NB, 4, P], F32, name="hp")
        zo = const.tile([P, NB, 4, P], F32, name="zo", tag="zo")
        ub = const.tile([P, 4, 4, P], BF16, name="ub")
        yg = const.tile([P, 4, P, 4], BF16, name="yg", align_bytes=64)
        st6 = const.tile([P, 2, NB, 6], F32, name="st6")
        mv = const.tile([P, 2, 2], F32, name="mv")
        rstd_a = const.tile([P, 1], F32, name="rstd_a")
        rstd_b = const.tile([P, 1], F32, name="rstd_b")

        def first_pass(idx, nb, rhs):
            s, g = groups[idx]
            bank = acc_a[nb] if idx < 12 else acc_b[nb]
            nc.tensor.matmul_mx(
                out=bank[:],
                lhsT=aw[:, s, g * P : (g + 1) * P].bitcast(FP8X4),
                lhsT_scale=asc[:, s, g * P : (g + 1) * P],
                rhs=rhs.bitcast(FP8X4),
                rhs_scale=planes[4 * g : P, s, nb * CB : (nb + 1) * CB],
                start=(idx == 0 or idx == 12),
                stop=(idx == 11 or idx == 19),
            )

        def flat(tile4, nb):
            return tile4[:, nb].rearrange("w t p -> w (t p)")

        def statistics(ph, rstd):
            nc.vector.bn_aggr(out=mv[:, ph, :], in_=st6[:, ph].rearrange("w a c -> w (a c)"))
            nc.scalar.activation(
                out=rstd[:], in_=mv[:, ph, 1:2], func=ACT.Abs_reciprocal_sqrt, bias=eps[:], scale=1.0
            )

        def normalise(ph, rstd, dst, nb):
            nc.vector.tensor_scalar(
                out=flat(dst, nb),
                in0=flat(hp, nb),
                scalar1=mv[:, ph, 0:1],
                scalar2=rstd[:],
                op0=ALU.subtract,
                op1=ALU.mult,
            )

        for idx in range(18):
            if idx == 12:
                for nb in range(NB):
                    acc_b.append(auxp.tile([P, CB], F32, name="accb%d" % nb, tag="aux%d" % nb))
            for nb in range(NB):
                first_pass(idx, nb, tiles[idx][:, nb * CB : (nb + 1) * CB])
            state["big_out"] -= 1
            issue_loads()
            if idx == 6:
                spread_bias(0)
            if idx == 8:
                spread_bias(1)
            if idx == 11:
                for nb in range(NB):
                    nc.vector.tensor_tensor(
                        out=hp[:, nb],
                        in0=acc_a[nb][:].rearrange("w (p t) -> w t p", t=4),
                        in1=b1p[:, nb],
                        op=ALU.add,
                    )
                    nc.vector.bn_stats(out=st6[:, 0, nb, :], in_=flat(hp, nb))
                statistics(0, rstd_a)
                for nb in range(NB):
                    normalise(0, rstd_a, zo, nb)
            if idx == EARLY_AT:
                for g in range(4):
                    tt = accp.tile([P, 4, P], F32, name="tta", tag="acc%d" % g)
                    for t in range(4):
                        nc.tensor.transpose(tt[:, t, :], zo[:, g, t, :], ident[:])
                    for t in range(4):
                        nc.scalar.activation(
                            out=ub[:, g, t, :],
                            in_=tt[:, t, :],
                            func=ACT.Relu,
                            scale=prm[:, g, 0, t : t + 1],
                            bias=prm[:, g, 1, t : t + 1],
                        )
                    nc.vector.tensor_copy(
                        out=yg[:, g], in_=ub[:, g].rearrange("p t w -> p w t")
                    )
        hd = const.tile([P, 4, 2, 8, 4], F32, name="hd")
        dt = const.tile([P, 4, 2, 8, 4], F32, name="dt")
        yw = const.tile([P, 4, P], U32, name="yw", align_bytes=64)
        ys = const.tile([P, 4, P], U8, name="ys", align_bytes=64)

        def raw_transposes(g):
            tt = auxp.tile([P, 4, P], F32, name="ttb", tag="aux%d" % g)
            for t in range(4):
                nc.tensor.transpose(tt[:, t, :], hp[:, g, t, :], ident[:])
            src = tt[:].rearrange("p t (b m) -> p b m t", b=2)[:, :, 0:64:9, :]
            if g < 3:
                nc.scalar.copy(out=hd[:, g], in_=src)
            else:
                nc.vector.tensor_copy(out=hd[:, g], in_=src)

        ssum = const.tile([P, NB], F32, name="ssum")
        qsum = const.tile([P, NB], F32, name="qsum")
        sq = const.tile([P, CB], BF16, name="sq")
        scr = const.tile([P, 2, NB], F32, name="scr")
        mu_b = const.tile([P, 1], F32, name="mu_b")
        ex2 = const.tile([P, 1], F32, name="ex2")
        nvar = const.tile([P, 1], F32, name="nvar")
        for nb in range(NB):
            first_pass(18, nb, tiles[18 + nb][:, 0, :])
            first_pass(19, nb, tiles[18 + nb][:, 1, :])
            nc.vector.scalar_tensor_tensor(
                out=hp[:, nb],
                in0=acc_b[nb][:].rearrange("w (p t) -> w t p", t=4),
                scalar=mv[:, 0, 0:1],
                in1=hp[:, nb],
                op0=ALU.subtract,
                op1=ALU.add,
                accum_out=ssum[:, nb : nb + 1],
            )
            nc.scalar.activation(
                out=sq[:], in_=flat(hp, nb), func=ACT.Square, accum_out=qsum[:, nb : nb + 1]
            )
            if nb >= 1:
                raw_transposes(nb - 1)
        nc.vector.tensor_scalar(
            out=scr[:, 0, 0:3], in0=qsum[:, 0:3], scalar1=1.0 / F, scalar2=EPS,
            op0=ALU.mult, op1=ALU.add, accum_out=ex2[:],
        )
        nc.vector.tensor_scalar(
            out=scr[:, 1, :], in0=ssum[:], scalar1=1.0 / F, scalar2=0.0,
            op0=ALU.mult, op1=ALU.add, accum_out=mu_b[:],
        )
        nc.vector.tensor_scalar(
            out=nvar[:], in0=mu_b[:], scalar1=mu_b[:], scalar2=ex2[:],
            op0=ALU.mult, op1=ALU.subtract,
        )
        raw_transposes(3)
        wm = accp.tile([P, CB], F32, name="wm", tag="acc3")

        def keep_warm(count):
            for i in range(count):
                nc.tensor.matmul(
                    wm[:], lhsT=sel[:, 0, :], rhs=br[:, 0:CB], start=True, stop=True
                )

        keep_warm(WARM[0])
        nc.scalar.activation(
            out=rstd_b[:], in_=qsum[:, 3:4], func=ACT.Abs_reciprocal_sqrt, bias=nvar[:], scale=-1.0 / F
        )
        tm = auxp.tile([P, P], F32, name="tm", tag="aux0")
        nc.tensor.transpose(tm[:], mu_b[:, 0:1].to_broadcast([P, P]), ident[:])
        keep_warm(WARM[1])
        tr = auxp.tile([P, P], F32, name="tr", tag="aux1")
        nc.tensor.transpose(tr[:], rstd_b[:, 0:1].to_broadcast([P, P]), ident[:])
        keep_warm(WARM[2])

        ot = const.tile([P, NB, CB], F32, name="ot", tag="zo")
        acc2 = [accp.tile([P, CB], F32, name="out%d" % nb, tag="acc%d" % nb) for nb in range(NB)]
        out_flat = out.rearrange("b n i j d -> (b n i j) d")

        def spread(g, v):
            return prm[:, g, v, :].unsqueeze(1).unsqueeze(1).to_broadcast([P, 2, 8, 4])

        def of_rows(ps):
            return (
                ps[:].rearrange("p (b m) -> p b m", b=2)[:, :, 0:64:9]
                .unsqueeze(3)
                .to_broadcast([P, 2, 8, 4])
            )

        def second_pass(g, nb):
            if g < 3:
                rhs = tiles[22 + g][:, nb * CB : (nb + 1) * CB]
            else:
                rhs = tiles[25 + nb][:]
            nc.tensor.matmul_mx(
                out=acc2[nb][:],
                lhsT=yw[:, g, :].bitcast(FP8X4),
                lhsT_scale=ys[:, g, :],
                rhs=rhs.bitcast(FP8X4),
                rhs_scale=planes[4 * g : P, 5, nb * CB : (nb + 1) * CB],
                start=(g == 0),
                stop=(g == 3),
            )

        for g in range(4):
            nc.vector.tensor_tensor(out=hd[:, g], in0=hd[:, g], in1=of_rows(tm), op=ALU.subtract)
        for g in range(4):
            nc.vector.tensor_tensor(out=hd[:, g], in0=hd[:, g], in1=spread(g, 0), op=ALU.mult)
        for g in range(4):
            nc.vector.tensor_tensor(out=dt[:, g], in0=hd[:, g], in1=of_rows(tr), op=ALU.mult)
        for g in range(4):
            nc.vector.tensor_tensor(out=dt[:, g], in0=dt[:, g], in1=spread(g, 3), op=ALU.add)
        for g in range(4):
            nc.vector.tensor_tensor(
                out=yg[:, g].rearrange("p (b m) t -> p b m t", b=2)[:, :, 0:64:9, :],
                in0=dt[:, g],
                in1=spread(g, 2),
                op=ALU.max,
            )
        for g in range(4):
            nc.vector.quantize_mx(
                out=yw[:, g, :].bitcast(FP8X4),
                scales=ys[:, g, :],
                in_=yg[:, g].rearrange("p w t -> p (w t)"),
            )
        for g in range(3):
            for nb in range(NB):
                second_pass(g, nb)
        for nb in range(NB):
            second_pass(3, nb)
            pieces = 2 if nb == NB - 1 else 1
            width = CB // pieces
            for h in range(pieces):
                cols = slice(h * width, (h + 1) * width)
                nc.vector.tensor_tensor(
                    out=ot[:, nb, cols], in0=acc2[nb][:, cols], in1=b2b[:, nb, cols], op=ALU.add
                )
                nc.sync.dma_start(
                    out=out_flat[:, nb * CB + h * width : nb * CB + (h + 1) * width],
                    in_=ot[:, nb, cols],
                )
